import numpy as np
import ml_dtypes

BF16 = ml_dtypes.bfloat16


def bf(x):
    return np.asarray(x, np.float32).astype(BF16)


def f32(x):
    return np.asarray(x, np.float32)


def f64(x):
    return np.asarray(x).astype(np.float64)


def striped(idx):
    return np.tile(idx.reshape(-1, 16).T, (8, 1))


C, S, N, H = 256, 1024, 2048, 512
LN_EPS = 1e-5


def setup_inputs():
    return {
        "codebook": bf(np.random.standard_normal((C, S))),
        "map_pos": bf(0.5 * np.random.standard_normal((C, N))),
        "ego_pos": f32(0.5 * np.random.standard_normal((C, N))),
        "w0": bf(np.random.standard_normal((C, H)) / np.sqrt(C)),
        "b0": f32(0.1 * np.random.standard_normal((H, 1))),
        "gain": f32(1.0 + 0.1 * np.random.standard_normal((H, 1))),
        "shift": f32(0.1 * np.random.standard_normal((H, 1))),
        "w1": bf(np.random.standard_normal((H, C)) / np.sqrt(H)),
        "b1": f32(0.1 * np.random.standard_normal((C, 1))),
        "offs": striped(np.random.permutation(np.tile(np.arange(S), 2))[:N]),
    }


def reference(codebook, map_pos, ego_pos, w0, b0, gain, shift, w1, b1, offs):
    idx = offs[:16].T.reshape(-1)
    feat = f64(codebook)[:, idx] + f64(map_pos) + f64(ego_pos)
    u = f64(w0).T @ feat + f64(b0)
    mu = u.mean(axis=0, keepdims=True)
    var = np.square(u - mu).mean(axis=0, keepdims=True)
    m = np.maximum((u - mu) / np.sqrt(var + LN_EPS) * f64(gain) + f64(shift), 0.0)
    return f64(w1).T @ m + f64(b1)

@@ -1,0 +1,188 @@
+from contextlib import ExitStack
+
+import concourse.mybir as mybir
+from concourse.masks import make_identity
+
+BF16 = mybir.dt.bfloat16
+F32 = mybir.dt.float32
+U16 = mybir.dt.uint16
+ALU = mybir.AluOpType
+ACT = mybir.ActivationFunctionType
+
+P = 128
+C, S, N, H = 256, 1024, 2048, 512
+CB = C // P
+HB = H // P
+CHUNK = 512
+NCH = N // CHUNK
+TB = CHUNK // P
+NT = N // P
+LN_EPS = 1e-5
+
+FLOPS = 2 * N * C * H + 2 * N * H * C
+
+
+def tile_maplatentencoder_kernel(
+    tc, codebook, map_pos, ego_pos, w0, b0, gain, shift, w1, b1, offs, out
+):
+    nc = tc.nc
+    with ExitStack() as ctx:
+        held = ctx.enter_context(tc.tile_pool(name="held", bufs=1))
+        loads = ctx.enter_context(tc.tile_pool(name="loads", bufs=NCH))
+        work = ctx.enter_context(tc.tile_pool(name="work", bufs=2))
+        small = ctx.enter_context(tc.tile_pool(name="small", bufs=4))
+        psum_u = ctx.enter_context(tc.psum_pool(name="psum_u", bufs=2))
+        psum_t = ctx.enter_context(tc.psum_pool(name="psum_t", bufs=1))
+        psum_o = ctx.enter_context(tc.psum_pool(name="psum_o", bufs=2))
+
+        offsets = held.tile([P, N // 16], U16, name="offsets")
+        nc.sync.dma_start(offsets[:], offs)
+        code_bf = held.tile([P, CB, S], BF16, name="code_bf")
+        nc.sync.dma_start(code_bf[:], codebook.rearrange("(cb p) s -> p cb s", p=P))
+        b0_all = held.tile([P, H], F32, name="b0_all")
+        nc.scalar.dma_start(b0_all[:], b0.rearrange("h o -> (h o)").partition_broadcast(P))
+        map_view = map_pos.rearrange("(cb p) n -> p cb n", p=P)
+        ego_view = ego_pos.rearrange("(cb p) n -> p cb n", p=P)
+        map_sb, ego_sb = [], []
+
+        def load_chunk(ch):
+            tokens = slice(ch * CHUNK, (ch + 1) * CHUNK)
+            map_t = loads.tile([P, CB, CHUNK], BF16, name="map_t")
+            nc.scalar.dma_start(map_t[:], map_view[:, :, tokens])
+            ego_t = loads.tile([P, CB, CHUNK], F32, name="ego_t")
+            nc.sync.dma_start(ego_t[:], ego_view[:, :, tokens])
+            map_sb.append(map_t)
+            ego_sb.append(ego_t)
+
+        load_chunk(0)
+        w0_sb = held.tile([P, CB, H], BF16, name="w0_sb")
+        nc.scalar.dma_start(w0_sb[:], w0.rearrange("(cb p) h -> p cb h", p=P))
+        rows = held.tile([P, P], F32, name="rows")
+        nc.vector.memset(rows[:], 0.0)
+        nc.scalar.dma_start(rows[0:HB, :], gain.rearrange("(b p) o -> b (p o)", p=P))
+        nc.scalar.dma_start(rows[HB : 2 * HB, :], shift.rearrange("(b p) o -> b (p o)", p=P))
+        nc.scalar.dma_start(rows[2 * HB : 2 * HB + CB, :], b1.rearrange("(b p) o -> b (p o)", p=P))
+        w1_sb = held.tile([P, HB, C], BF16, name="w1_sb")
+        nc.scalar.dma_start(w1_sb[:], w1.rearrange("(hb p) d -> p hb d", p=P))
+        for ch in range(1, NCH):
+            load_chunk(ch)
+
+        ident = held.tile([P, P], F32, name="ident")
+        make_identity(nc, ident[:])
+        ones = held.tile([P, P], BF16, name="ones")
+        nc.vector.memset(ones[:], 1.0)
+        eps = held.tile([P, 1], F32, name="eps")
+        nc.vector.memset(eps[:], LN_EPS)
+
+        hi = held.tile([P, H], BF16, name="hi")
+        nc.vector.tensor_copy(hi[:], b0_all[:])
+        rest1 = held.tile([P, H], F32, name="rest1")
+        nc.vector.tensor_tensor(rest1[:], b0_all[:], hi[:], ALU.subtract)
+        mid = held.tile([P, H], BF16, name="mid")
+        nc.vector.tensor_copy(mid[:], rest1[:])
+        rest2 = held.tile([P, H], F32, name="rest2")
+        nc.vector.tensor_tensor(rest2[:], rest1[:], mid[:], ALU.subtract)
+        row0 = held.tile([P, H], BF16, name="row0")
+        nc.vector.tensor_scalar(row0[:], hi[:], ident[:, 0:1], None, ALU.mult)
+        row01 = held.tile([P, H], BF16, name="row01")
+        nc.vector.scalar_tensor_tensor(row01[:], mid[:], ident[:, 1:2], row0[:], ALU.mult, ALU.add)
+        b0_rows = held.tile([P, H], BF16, name="b0_rows")
+        nc.vector.scalar_tensor_tensor(b0_rows[:], rest2[:], ident[:, 2:3], row01[:], ALU.mult, ALU.add)
+
+        window = []
+        for cb in range(CB):
+            code_f = held.tile([P, S], F32, name=f"code_f{cb}")
+            nc.vector.tensor_copy(code_f[:], code_bf[:, cb, :])
+            window.append(code_f)
+
+        cols_ps = psum_o.tile([P, CHUNK], F32, tag="o_ps", name="cols_ps")
+        nc.tensor.transpose(cols_ps[:, 0:P], rows[:], ident[:])
+        cols = held.tile([P, 2 * HB + CB], F32, name="cols")
+        nc.vector.tensor_copy(cols[:], cols_ps[:, 0 : 2 * HB + CB])
+
+        feats = {}
+        normed = {}
+        flipped = {}
+
+        def make_feat(ch):
+            pos = work.tile([P, CB, CHUNK], F32, name="pos")
+            feat_f = work.tile([P, CB, CHUNK], F32, name="feat_f")
+            feat = work.tile([P, CB, CHUNK], BF16, name="feat")
+            piece = offsets[:, ch * (CHUNK // 16) : (ch + 1) * (CHUNK // 16)]
+            for cb in range(CB):
+                nc.gpsimd.tensor_tensor(pos[:, cb, :], map_sb[ch][:, cb, :], ego_sb[ch][:, cb, :], ALU.add)
+                nc.vector.tensor_tensor(
+                    feat_f[:, cb, :], window[cb][:].indirect(piece), pos[:, cb, :], ALU.add
+                )
+                nc.gpsimd.tensor_copy(feat[:, cb, :], feat_f[:, cb, :])
+            feats[ch] = feat
+
+        def hidden(t):
+            feat = feats[t // TB]
+            tokens = slice((t % TB) * P, (t % TB + 1) * P)
+            u_ps = psum_u.tile([P, H], F32, name="u_ps")
+            nc.tensor.matmul(u_ps[:], ones[:], b0_rows[:], start=True, stop=False)
+            for cb in range(CB):
+                nc.tensor.matmul(
+                    u_ps[:], feat[:, cb, tokens], w0_sb[:, cb, :], start=False, stop=(cb == CB - 1)
+                )
+            stats = small.tile([P, 6], F32, name="stats")
+            nc.vector.bn_stats(stats[:], u_ps[:])
+            mean_var = small.tile([P, 2], F32, name="mean_var")
+            nc.vector.bn_aggr(mean_var[:], stats[:])
+            neg_mean = small.tile([P, 1], F32, name="neg_mean")
+            nc.vector.tensor_scalar_mul(neg_mean[:], mean_var[:, 0:1], -1.0)
+            rstd = small.tile([P, 1], F32, name="rstd")
+            nc.scalar.activation(rstd[:], mean_var[:, 1:2], ACT.Abs_reciprocal_sqrt, bias=eps[:])
+            offset = small.tile([P, 1], F32, name="offset")
+            nc.scalar.activation(offset[:], neg_mean[:], ACT.Identity, scale=rstd[:])
+            x_hat = work.tile([P, H], F32, name="x_hat")
+            nc.scalar.activation(x_hat[:], u_ps[:], ACT.Identity, bias=offset[:], scale=rstd[:])
+            normed[t] = x_hat
+
+        def flip(t):
+            if t % TB == 0:
+                flipped[t // TB] = [
+                    psum_t.tile([P, CHUNK], F32, name=f"flip{hb}") for hb in range(HB)
+                ]
+            tokens = slice((t % TB) * P, (t % TB + 1) * P)
+            for hb in range(HB):
+                nc.tensor.transpose(
+                    flipped[t // TB][hb][:, tokens], normed[t][:, hb * P : (hb + 1) * P], ident[:]
+                )
+
+        def finish(ch):
+            m = work.tile([P, HB, CHUNK], BF16, name="m")
+            o_ps = [psum_o.tile([P, CHUNK], F32, tag="o_ps", name=f"o_ps{db}") for db in range(CB)]
+            for hb in range(HB):
+                nc.scalar.activation(
+                    m[:, hb, :],
+                    flipped[ch][hb][:],
+                    ACT.Relu,
+                    bias=cols[:, HB + hb : HB + hb + 1],
+                    scale=cols[:, hb : hb + 1],
+                )
+                for db in range(CB):
+                    nc.tensor.matmul(
+                        o_ps[db][:],
+                        w1_sb[:, hb, db * P : (db + 1) * P],
+                        m[:, hb, :],
+                        start=(hb == 0),
+                        stop=(hb == HB - 1),
+                    )
+            for db in range(CB):
+                o_sb = work.tile([P, CHUNK], F32, name="o_sb")
+                nc.vector.tensor_scalar_add(o_sb[:], o_ps[db][:], cols[:, 2 * HB + db : 2 * HB + db + 1])
+                nc.sync.dma_start(out[db * P : (db + 1) * P, ch * CHUNK : (ch + 1) * CHUNK], o_sb[:])
+
+        make_feat(0)
+        for t in range(NT):
+            if t % TB == 0 and t // TB + 1 < NCH:
+                make_feat(t // TB + 1)
+            hidden(t)
+            if t >= 1:
+                flip(t - 1)
+                if t % TB == 0:
+                    finish(t // TB - 1)
+        flip(NT - 1)
+        finish(NCH - 1)

@@ -13,13 +13,21 @@ P = 128
 C, S, N, H = 256, 1024, 2048, 512
 CB = C // P
 HB = H // P
-CHUNK = 512
-NCH = N // CHUNK
-TB = CHUNK // P
 NT = N // P
+PIECE = 256
+NQ = N // PIECE
+BLOCKS_IN_PIECE = PIECE // P
+CHUNK = 512
+BLOCKS_IN_CHUNK = CHUNK // P
 LN_EPS = 1e-5
+AHEAD = 3
+FEAT_AHEAD = 7
 
 FLOPS = 2 * N * C * H + 2 * N * H * C
+
+
+def as_rows(vector):
+    return vector.rearrange("(b p) o -> b (p o)", p=P)
 
 
 def tile_maplatentencoder_kernel(
@@ -28,161 +36,200 @@ def tile_maplatentencoder_kernel(
     nc = tc.nc
     with ExitStack() as ctx:
         held = ctx.enter_context(tc.tile_pool(name="held", bufs=1))
-        loads = ctx.enter_context(tc.tile_pool(name="loads", bufs=NCH))
-        work = ctx.enter_context(tc.tile_pool(name="work", bufs=2))
-        small = ctx.enter_context(tc.tile_pool(name="small", bufs=4))
-        psum_u = ctx.enter_context(tc.psum_pool(name="psum_u", bufs=2))
-        psum_t = ctx.enter_context(tc.psum_pool(name="psum_t", bufs=1))
+        loads = ctx.enter_context(tc.tile_pool(name="loads", bufs=NQ))
+        work = ctx.enter_context(tc.tile_pool(name="work", bufs=4))
+        small = ctx.enter_context(tc.tile_pool(name="small", bufs=6))
+        psum_u = ctx.enter_context(tc.psum_pool(name="psum_u", bufs=4))
+        psum_t = ctx.enter_context(tc.psum_pool(name="psum_t", bufs=2))
         psum_o = ctx.enter_context(tc.psum_pool(name="psum_o", bufs=2))
 
         offsets = held.tile([P, N // 16], U16, name="offsets")
         nc.sync.dma_start(offsets[:], offs)
-        code_bf = held.tile([P, CB, S], BF16, name="code_bf")
-        nc.sync.dma_start(code_bf[:], codebook.rearrange("(cb p) s -> p cb s", p=P))
-        b0_all = held.tile([P, H], F32, name="b0_all")
-        nc.scalar.dma_start(b0_all[:], b0.rearrange("h o -> (h o)").partition_broadcast(P))
+        code_bf = []
+        for cb in range(CB):
+            code_t = held.tile([P, S], BF16, name=f"code_bf{cb}")
+            nc.scalar.dma_start(code_t[:], codebook[cb * P : (cb + 1) * P, :])
+            code_bf.append(code_t)
+        w0_sb = held.tile([P, CB, H], BF16, name="w0_sb")
+        nc.scalar.dma_start(w0_sb[:], w0.rearrange("(cb p) h -> p cb h", p=P))
+        b0_as_rows = held.tile([P, P], F32, name="b0_as_rows")
+        nc.gpsimd.memset(b0_as_rows[:], 0.0)
+        nc.gpsimd.dma_start(b0_as_rows[0:HB, :], as_rows(b0))
+        rows = held.tile([P, P], F32, name="rows")
+        nc.gpsimd.memset(rows[:], 0.0)
+
         map_view = map_pos.rearrange("(cb p) n -> p cb n", p=P)
         ego_view = ego_pos.rearrange("(cb p) n -> p cb n", p=P)
         map_sb, ego_sb = [], []
 
-        def load_chunk(ch):
-            tokens = slice(ch * CHUNK, (ch + 1) * CHUNK)
-            map_t = loads.tile([P, CB, CHUNK], BF16, name="map_t")
-            nc.scalar.dma_start(map_t[:], map_view[:, :, tokens])
-            ego_t = loads.tile([P, CB, CHUNK], F32, name="ego_t")
+        def load_piece(q):
+            tokens = slice(q * PIECE, (q + 1) * PIECE)
+            ego_t = loads.tile([P, CB, PIECE], F32, name="ego_t")
             nc.sync.dma_start(ego_t[:], ego_view[:, :, tokens])
+            map_t = loads.tile([P, CB, PIECE], BF16, name="map_t")
+            nc.sync.dma_start(map_t[:], map_view[:, :, tokens])
             map_sb.append(map_t)
             ego_sb.append(ego_t)
 
-        load_chunk(0)
-        w0_sb = held.tile([P, CB, H], BF16, name="w0_sb")
-        nc.scalar.dma_start(w0_sb[:], w0.rearrange("(cb p) h -> p cb h", p=P))
-        rows = held.tile([P, P], F32, name="rows")
-        nc.vector.memset(rows[:], 0.0)
-        nc.scalar.dma_start(rows[0:HB, :], gain.rearrange("(b p) o -> b (p o)", p=P))
-        nc.scalar.dma_start(rows[HB : 2 * HB, :], shift.rearrange("(b p) o -> b (p o)", p=P))
-        nc.scalar.dma_start(rows[2 * HB : 2 * HB + CB, :], b1.rearrange("(b p) o -> b (p o)", p=P))
+        for q in range(3):
+            load_piece(q)
+        nc.sync.dma_start(rows[0:HB, :], as_rows(gain))
+        nc.sync.dma_start(rows[HB : 2 * HB, :], as_rows(shift))
+        nc.sync.dma_start(rows[2 * HB : 2 * HB + CB, :], as_rows(b1))
+        load_piece(3)
         w1_sb = held.tile([P, HB, C], BF16, name="w1_sb")
-        nc.scalar.dma_start(w1_sb[:], w1.rearrange("(hb p) d -> p hb d", p=P))
-        for ch in range(1, NCH):
-            load_chunk(ch)
+        nc.sync.dma_start(w1_sb[:], w1.rearrange("(hb p) d -> p hb d", p=P))
+        for q in range(4, NQ):
+            load_piece(q)
 
         ident = held.tile([P, P], F32, name="ident")
         make_identity(nc, ident[:])
+        ident_bf = held.tile([P, P], BF16, name="ident_bf")
+        make_identity(nc, ident_bf[:])
         ones = held.tile([P, P], BF16, name="ones")
         nc.vector.memset(ones[:], 1.0)
         eps = held.tile([P, 1], F32, name="eps")
         nc.vector.memset(eps[:], LN_EPS)
-
-        hi = held.tile([P, H], BF16, name="hi")
-        nc.vector.tensor_copy(hi[:], b0_all[:])
-        rest1 = held.tile([P, H], F32, name="rest1")
-        nc.vector.tensor_tensor(rest1[:], b0_all[:], hi[:], ALU.subtract)
-        mid = held.tile([P, H], BF16, name="mid")
-        nc.vector.tensor_copy(mid[:], rest1[:])
-        rest2 = held.tile([P, H], F32, name="rest2")
-        nc.vector.tensor_tensor(rest2[:], rest1[:], mid[:], ALU.subtract)
-        row0 = held.tile([P, H], BF16, name="row0")
-        nc.vector.tensor_scalar(row0[:], hi[:], ident[:, 0:1], None, ALU.mult)
-        row01 = held.tile([P, H], BF16, name="row01")
-        nc.vector.scalar_tensor_tensor(row01[:], mid[:], ident[:, 1:2], row0[:], ALU.mult, ALU.add)
         b0_rows = held.tile([P, H], BF16, name="b0_rows")
-        nc.vector.scalar_tensor_tensor(b0_rows[:], rest2[:], ident[:, 2:3], row01[:], ALU.mult, ALU.add)
+        nc.vector.memset(b0_rows[:], 0.0)
 
-        window = []
-        for cb in range(CB):
-            code_f = held.tile([P, S], F32, name=f"code_f{cb}")
-            nc.vector.tensor_copy(code_f[:], code_bf[:, cb, :])
-            window.append(code_f)
+        window = [held.tile([P, S], F32, name=f"window{cb}") for cb in range(CB)]
+        nc.vector.tensor_copy(window[0][:], code_bf[0][:])
+        nc.scalar.copy(window[1][:], code_bf[1][:])
 
-        cols_ps = psum_o.tile([P, CHUNK], F32, tag="o_ps", name="cols_ps")
-        nc.tensor.transpose(cols_ps[:, 0:P], rows[:], ident[:])
+        b0_cols = psum_t.tile([P, P], F32, tag="flipped", name="b0_cols")
+        nc.tensor.transpose(b0_cols[:], b0_as_rows[:], ident[:])
+        parts = held.tile([P, HB, 3], BF16, name="parts")
+        rest = held.tile([P, HB], F32, name="rest")
+        nc.vector.tensor_copy(parts[:, :, 0], b0_cols[:, 0:HB])
+        nc.vector.tensor_tensor(rest[:], b0_cols[:, 0:HB], parts[:, :, 0], ALU.subtract)
+        nc.vector.tensor_copy(parts[:, :, 1], rest[:])
+        nc.vector.tensor_tensor(parts[:, :, 2], rest[:], parts[:, :, 1], ALU.subtract)
+        b0_ps = psum_t.tile([P, H], F32, tag="flipped", name="b0_ps")
+        for hb in range(HB):
+            nc.tensor.matmul(
+                b0_ps[0:3, hb * P : (hb + 1) * P], parts[:, hb, :], ident_bf[:], start=True, stop=True
+            )
+        nc.scalar.copy(b0_rows[0:3, :], b0_ps[0:3, :])
+
+        pos_of, feat_f_of, feat_of = {}, {}, {}
+        u_of, mean_var_of, rstd_of, offset_of, x_hat_of, m_of, o_of = {}, {}, {}, {}, {}, {}, {}
         cols = held.tile([P, 2 * HB + CB], F32, name="cols")
-        nc.vector.tensor_copy(cols[:], cols_ps[:, 0 : 2 * HB + CB])
+        gain_col = [cols[:, hb : hb + 1] for hb in range(HB)]
+        shift_col = [cols[:, HB + hb : HB + hb + 1] for hb in range(HB)]
+        b1_col = [cols[:, 2 * HB + db : 2 * HB + db + 1] for db in range(CB)]
 
-        feats = {}
-        normed = {}
-        flipped = {}
+        def columns():
+            cols_ps = psum_t.tile([P, P], F32, tag="flipped", name="cols_ps")
+            nc.tensor.transpose(cols_ps[:], rows[:], ident[:])
+            nc.vector.tensor_copy(cols[:], cols_ps[:, 0 : 2 * HB + CB])
 
-        def make_feat(ch):
-            pos = work.tile([P, CB, CHUNK], F32, name="pos")
-            feat_f = work.tile([P, CB, CHUNK], F32, name="feat_f")
-            feat = work.tile([P, CB, CHUNK], BF16, name="feat")
-            piece = offsets[:, ch * (CHUNK // 16) : (ch + 1) * (CHUNK // 16)]
-            for cb in range(CB):
-                nc.gpsimd.tensor_tensor(pos[:, cb, :], map_sb[ch][:, cb, :], ego_sb[ch][:, cb, :], ALU.add)
-                nc.vector.tensor_tensor(
-                    feat_f[:, cb, :], window[cb][:].indirect(piece), pos[:, cb, :], ALU.add
-                )
-                nc.gpsimd.tensor_copy(feat[:, cb, :], feat_f[:, cb, :])
-            feats[ch] = feat
+        def add_positions(i):
+            q, cb = divmod(i, CB)
+            if q >= NQ:
+                return
+            if cb == 0:
+                pos_of[q] = work.tile([P, CB, PIECE], F32, name="pos")
+            nc.gpsimd.tensor_tensor(pos_of[q][:, cb, :], map_sb[q][:, cb, :], ego_sb[q][:, cb, :], ALU.add)
+
+        def look_up(i):
+            q, cb = divmod(i, CB)
+            if q >= NQ:
+                return
+            if cb == 0:
+                feat_f_of[q] = work.tile([P, CB, PIECE], F32, name="feat_f")
+            piece = offsets[:, q * (PIECE // 16) : (q + 1) * (PIECE // 16)]
+            nc.vector.tensor_tensor(
+                feat_f_of[q][:, cb, :], window[cb][:].indirect(piece), pos_of[q][:, cb, :], ALU.add
+            )
+            if cb == CB - 1:
+                feat_of[q] = work.tile([P, CB, PIECE], BF16, name="feat")
+                nc.gpsimd.tensor_copy(feat_of[q][:], feat_f_of[q][:])
+            add_positions(i + 2)
 
         def hidden(t):
-            feat = feats[t // TB]
-            tokens = slice((t % TB) * P, (t % TB + 1) * P)
+            if not 0 <= t < NT:
+                return
+            feat = feat_of[t // BLOCKS_IN_PIECE]
+            tokens = slice((t % BLOCKS_IN_PIECE) * P, (t % BLOCKS_IN_PIECE + 1) * P)
             u_ps = psum_u.tile([P, H], F32, name="u_ps")
-            nc.tensor.matmul(u_ps[:], ones[:], b0_rows[:], start=True, stop=False)
             for cb in range(CB):
-                nc.tensor.matmul(
-                    u_ps[:], feat[:, cb, tokens], w0_sb[:, cb, :], start=False, stop=(cb == CB - 1)
-                )
+                nc.tensor.matmul(u_ps[:], feat[:, cb, tokens], w0_sb[:, cb, :], start=(cb == 0), stop=False)
+            nc.tensor.matmul(u_ps[:], ones[:], b0_rows[:], start=False, stop=True)
             stats = small.tile([P, 6], F32, name="stats")
             nc.vector.bn_stats(stats[:], u_ps[:])
             mean_var = small.tile([P, 2], F32, name="mean_var")
             nc.vector.bn_aggr(mean_var[:], stats[:])
-            neg_mean = small.tile([P, 1], F32, name="neg_mean")
-            nc.vector.tensor_scalar_mul(neg_mean[:], mean_var[:, 0:1], -1.0)
             rstd = small.tile([P, 1], F32, name="rstd")
             nc.scalar.activation(rstd[:], mean_var[:, 1:2], ACT.Abs_reciprocal_sqrt, bias=eps[:])
-            offset = small.tile([P, 1], F32, name="offset")
-            nc.scalar.activation(offset[:], neg_mean[:], ACT.Identity, scale=rstd[:])
+            u_of[t], mean_var_of[t], rstd_of[t] = u_ps, mean_var, rstd
+
+        def offset(t):
+            if not 0 <= t < NT:
+                return
+            minus = small.tile([P, 1], F32, name="minus")
+            nc.vector.tensor_scalar(minus[:], mean_var_of[t][:, 0:1], rstd_of[t][:], -1.0, ALU.mult, ALU.mult)
+            offset_of[t] = minus
+
+        def normalise(t):
+            if not 0 <= t < NT:
+                return
             x_hat = work.tile([P, H], F32, name="x_hat")
-            nc.scalar.activation(x_hat[:], u_ps[:], ACT.Identity, bias=offset[:], scale=rstd[:])
-            normed[t] = x_hat
+            nc.scalar.activation(x_hat[:], u_of[t][:], ACT.Identity, bias=offset_of[t][:], scale=rstd_of[t][:])
+            x_hat_of[t] = x_hat
 
-        def flip(t):
-            if t % TB == 0:
-                flipped[t // TB] = [
-                    psum_t.tile([P, CHUNK], F32, name=f"flip{hb}") for hb in range(HB)
-                ]
-            tokens = slice((t % TB) * P, (t % TB + 1) * P)
+        def activate(t):
+            if not 0 <= t < NT:
+                return
+            ch = t // BLOCKS_IN_CHUNK
+            if t % BLOCKS_IN_CHUNK == 0:
+                m_of[ch] = work.tile([P, HB, CHUNK], BF16, name="m")
+            tokens = slice((t % BLOCKS_IN_CHUNK) * P, (t % BLOCKS_IN_CHUNK + 1) * P)
+            flipped = psum_t.tile([P, HB, P], F32, tag="flipped", name="flipped")
             for hb in range(HB):
-                nc.tensor.transpose(
-                    flipped[t // TB][hb][:, tokens], normed[t][:, hb * P : (hb + 1) * P], ident[:]
-                )
-
-        def finish(ch):
-            m = work.tile([P, HB, CHUNK], BF16, name="m")
-            o_ps = [psum_o.tile([P, CHUNK], F32, tag="o_ps", name=f"o_ps{db}") for db in range(CB)]
+                nc.tensor.transpose(flipped[:, hb, :], x_hat_of[t][:, hb * P : (hb + 1) * P], ident[:])
             for hb in range(HB):
                 nc.scalar.activation(
-                    m[:, hb, :],
-                    flipped[ch][hb][:],
-                    ACT.Relu,
-                    bias=cols[:, HB + hb : HB + hb + 1],
-                    scale=cols[:, hb : hb + 1],
+                    m_of[ch][:, hb, tokens], flipped[:, hb, :], ACT.Relu, bias=shift_col[hb], scale=gain_col[hb]
                 )
-                for db in range(CB):
-                    nc.tensor.matmul(
-                        o_ps[db][:],
-                        w1_sb[:, hb, db * P : (db + 1) * P],
-                        m[:, hb, :],
-                        start=(hb == 0),
-                        stop=(hb == HB - 1),
-                    )
-            for db in range(CB):
-                o_sb = work.tile([P, CHUNK], F32, name="o_sb")
-                nc.vector.tensor_scalar_add(o_sb[:], o_ps[db][:], cols[:, 2 * HB + db : 2 * HB + db + 1])
-                nc.sync.dma_start(out[db * P : (db + 1) * P, ch * CHUNK : (ch + 1) * CHUNK], o_sb[:])
 
-        make_feat(0)
-        for t in range(NT):
-            if t % TB == 0 and t // TB + 1 < NCH:
-                make_feat(t // TB + 1)
-            hidden(t)
-            if t >= 1:
-                flip(t - 1)
-                if t % TB == 0:
-                    finish(t // TB - 1)
-        flip(NT - 1)
-        finish(NCH - 1)
+        def project(j):
+            if not 0 <= j < NT:
+                return
+            ch, hb = divmod(j, HB)
+            if hb == 0:
+                o_of[ch] = [psum_o.tile([P, CHUNK], F32, tag="o_ps", name=f"o_ps{db}") for db in range(CB)]
+            for db in range(CB):
+                nc.tensor.matmul(
+                    o_of[ch][db][:],
+                    w1_sb[:, hb, db * P : (db + 1) * P],
+                    m_of[ch][:, hb, :],
+                    start=(hb == 0),
+                    stop=(hb == HB - 1),
+                )
+            if hb == HB - 1:
+                for db in range(CB):
+                    o_sb = work.tile([P, CHUNK], F32, name="o_sb")
+                    if db == 0:
+                        nc.vector.tensor_scalar_add(o_sb[:], o_of[ch][db][:], b1_col[db])
+                    else:
+                        nc.scalar.activation(o_sb[:], o_of[ch][db][:], ACT.Identity, bias=b1_col[db])
+                    nc.sync.dma_start(out[db * P : (db + 1) * P, ch * CHUNK : (ch + 1) * CHUNK], o_sb[:])
+
+        def step(k):
+            normalise(k + AHEAD - 1)
+            hidden(k + AHEAD)
+            look_up(k + FEAT_AHEAD)
+            offset(k + AHEAD)
+            activate(k)
+            project(k - BLOCKS_IN_CHUNK)
+
+        add_positions(0)
+        add_positions(1)
+        for i in range(FEAT_AHEAD - AHEAD):
+            look_up(i)
+        for k in range(-AHEAD, 0):
+            step(k)
+        columns()
+        for k in range(0, NT + BLOCKS_IN_CHUNK):
+            step(k)

@@ -21,6 +21,8 @@ CHUNK = 512
 BLOCKS_IN_CHUNK = CHUNK // P
 LN_EPS = 1e-5
 AHEAD = 3
+BEHIND = 6
+PER_STEP = CB * HB // BLOCKS_IN_CHUNK
 FEAT_AHEAD = 7
 
 FLOPS = 2 * N * C * H + 2 * N * H * C
@@ -43,20 +45,16 @@ def tile_maplatentencoder_kernel(
         psum_t = ctx.enter_context(tc.psum_pool(name="psum_t", bufs=2))
         psum_o = ctx.enter_context(tc.psum_pool(name="psum_o", bufs=2))
 
-        offsets = held.tile([P, N // 16], U16, name="offsets")
-        nc.sync.dma_start(offsets[:], offs)
-        code_bf = []
-        for cb in range(CB):
-            code_t = held.tile([P, S], BF16, name=f"code_bf{cb}")
-            nc.scalar.dma_start(code_t[:], codebook[cb * P : (cb + 1) * P, :])
-            code_bf.append(code_t)
-        w0_sb = held.tile([P, CB, H], BF16, name="w0_sb")
-        nc.scalar.dma_start(w0_sb[:], w0.rearrange("(cb p) h -> p cb h", p=P))
         b0_as_rows = held.tile([P, P], F32, name="b0_as_rows")
         nc.gpsimd.memset(b0_as_rows[:], 0.0)
-        nc.gpsimd.dma_start(b0_as_rows[0:HB, :], as_rows(b0))
         rows = held.tile([P, P], F32, name="rows")
         nc.gpsimd.memset(rows[:], 0.0)
+        code_bf = [held.tile([P, S], BF16, name=f"code_bf{cb}") for cb in range(CB)]
+        nc.scalar.dma_start(code_bf[0][:], codebook[0:P, :])
+        nc.scalar.dma_start(b0_as_rows[0:HB, :], as_rows(b0))
+        nc.scalar.dma_start(code_bf[1][:], codebook[P : 2 * P, :])
+        w0_sb = held.tile([P, CB, H], BF16, name="w0_sb")
+        nc.scalar.dma_start(w0_sb[:], w0.rearrange("(cb p) h -> p cb h", p=P))
 
         map_view = map_pos.rearrange("(cb p) n -> p cb n", p=P)
         ego_view = ego_pos.rearrange("(cb p) n -> p cb n", p=P)
@@ -71,8 +69,11 @@ def tile_maplatentencoder_kernel(
             map_sb.append(map_t)
             ego_sb.append(ego_t)
 
-        for q in range(3):
-            load_piece(q)
+        load_piece(0)
+        offsets = held.tile([P, N // 16], U16, name="offsets")
+        nc.sync.dma_start(offsets[:], offs)
+        load_piece(1)
+        load_piece(2)
         nc.sync.dma_start(rows[0:HB, :], as_rows(gain))
         nc.sync.dma_start(rows[HB : 2 * HB, :], as_rows(shift))
         nc.sync.dma_start(rows[2 * HB : 2 * HB + CB, :], as_rows(b1))
@@ -196,24 +197,24 @@ def tile_maplatentencoder_kernel(
         def project(j):
             if not 0 <= j < NT:
                 return
-            ch, hb = divmod(j, HB)
-            if hb == 0:
-                o_of[ch] = [psum_o.tile([P, CHUNK], F32, tag="o_ps", name=f"o_ps{db}") for db in range(CB)]
-            for db in range(CB):
+            ch, part = divmod(j, BLOCKS_IN_CHUNK)
+            for n in range(part * PER_STEP, (part + 1) * PER_STEP):
+                db, hb = divmod(n, HB)
+                if hb == 0:
+                    o_of[db] = psum_o.tile([P, CHUNK], F32, name="o_ps")
                 nc.tensor.matmul(
-                    o_of[ch][db][:],
+                    o_of[db][:],
                     w1_sb[:, hb, db * P : (db + 1) * P],
                     m_of[ch][:, hb, :],
                     start=(hb == 0),
                     stop=(hb == HB - 1),
                 )
-            if hb == HB - 1:
-                for db in range(CB):
+                if hb == HB - 1:
                     o_sb = work.tile([P, CHUNK], F32, name="o_sb")
                     if db == 0:
-                        nc.vector.tensor_scalar_add(o_sb[:], o_of[ch][db][:], b1_col[db])
+                        nc.vector.tensor_scalar_add(o_sb[:], o_of[db][:], b1_col[db])
                     else:
-                        nc.scalar.activation(o_sb[:], o_of[ch][db][:], ACT.Identity, bias=b1_col[db])
+                        nc.scalar.activation(o_sb[:], o_of[db][:], ACT.Identity, bias=b1_col[db])
                     nc.sync.dma_start(out[db * P : (db + 1) * P, ch * CHUNK : (ch + 1) * CHUNK], o_sb[:])
 
         def step(k):
@@ -222,7 +223,7 @@ def tile_maplatentencoder_kernel(
             look_up(k + FEAT_AHEAD)
             offset(k + AHEAD)
             activate(k)
-            project(k - BLOCKS_IN_CHUNK)
+            project(k - BEHIND)
 
         add_positions(0)
         add_positions(1)
@@ -231,5 +232,5 @@ def tile_maplatentencoder_kernel(
         for k in range(-AHEAD, 0):
             step(k)
         columns()
-        for k in range(0, NT + BLOCKS_IN_CHUNK):
+        for k in range(0, NT + BEHIND):
             step(k)

@@ -145,7 +145,7 @@ def tile_maplatentencoder_kernel(
             )
             if cb == CB - 1:
                 feat_of[q] = work.tile([P, CB, PIECE], BF16, name="feat")
-                nc.gpsimd.tensor_copy(feat_of[q][:], feat_f_of[q][:])
+                nc.vector.tensor_copy(feat_of[q][:], feat_f_of[q][:])
             add_positions(i + 2)
 
         def hidden(t):

@@ -52,7 +52,6 @@ def tile_maplatentencoder_kernel(
         code_bf = [held.tile([P, S], BF16, name=f"code_bf{cb}") for cb in range(CB)]
         nc.scalar.dma_start(code_bf[0][:], codebook[0:P, :])
         nc.scalar.dma_start(b0_as_rows[0:HB, :], as_rows(b0))
-        nc.scalar.dma_start(code_bf[1][:], codebook[P : 2 * P, :])
         w0_sb = held.tile([P, CB, H], BF16, name="w0_sb")
         nc.scalar.dma_start(w0_sb[:], w0.rearrange("(cb p) h -> p cb h", p=P))
 
@@ -69,6 +68,7 @@ def tile_maplatentencoder_kernel(
             map_sb.append(map_t)
             ego_sb.append(ego_t)
 
+        nc.sync.dma_start(code_bf[1][:], codebook[P : 2 * P, :])
         load_piece(0)
         offsets = held.tile([P, N // 16], U16, name="offsets")
         nc.sync.dma_start(offsets[:], offs)

@@ -20,10 +20,7 @@ BLOCKS_IN_PIECE = PIECE // P
 CHUNK = 512
 BLOCKS_IN_CHUNK = CHUNK // P
 LN_EPS = 1e-5
-AHEAD = 3
-BEHIND = 6
 PER_STEP = CB * HB // BLOCKS_IN_CHUNK
-FEAT_AHEAD = 7
 
 FLOPS = 2 * N * C * H + 2 * N * H * C
 
@@ -114,7 +111,7 @@ def tile_maplatentencoder_kernel(
         nc.scalar.copy(b0_rows[0:3, :], b0_ps[0:3, :])
 
         pos_of, feat_f_of, feat_of = {}, {}, {}
-        u_of, mean_var_of, rstd_of, offset_of, x_hat_of, m_of, o_of = {}, {}, {}, {}, {}, {}, {}
+        u_of, stats_of, mean_var_of, rstd_of, offset_of, x_hat_of, flipped_of, m_of, o_of = {}, {}, {}, {}, {}, {}, {}, {}, {}
         cols = held.tile([P, 2 * HB + CB], F32, name="cols")
         gain_col = [cols[:, hb : hb + 1] for hb in range(HB)]
         shift_col = [cols[:, HB + hb : HB + hb + 1] for hb in range(HB)]
@@ -127,7 +124,7 @@ def tile_maplatentencoder_kernel(
 
         def add_positions(i):
             q, cb = divmod(i, CB)
-            if q >= NQ:
+            if not 0 <= q < NQ:
                 return
             if cb == 0:
                 pos_of[q] = work.tile([P, CB, PIECE], F32, name="pos")
@@ -135,7 +132,7 @@ def tile_maplatentencoder_kernel(
 
         def look_up(i):
             q, cb = divmod(i, CB)
-            if q >= NQ:
+            if not 0 <= q < NQ:
                 return
             if cb == 0:
                 feat_f_of[q] = work.tile([P, CB, PIECE], F32, name="feat_f")
@@ -143,41 +140,64 @@ def tile_maplatentencoder_kernel(
             nc.vector.tensor_tensor(
                 feat_f_of[q][:, cb, :], window[cb][:].indirect(piece), pos_of[q][:, cb, :], ALU.add
             )
-            if cb == CB - 1:
-                feat_of[q] = work.tile([P, CB, PIECE], BF16, name="feat")
-                nc.vector.tensor_copy(feat_of[q][:], feat_f_of[q][:])
-            add_positions(i + 2)
+
+        def round_feat(i):
+            q, cb = divmod(i, CB)
+            if not 0 <= q < NQ or cb != CB - 1:
+                return
+            feat_of[q] = work.tile([P, CB, PIECE], BF16, name="feat")
+            nc.vector.tensor_copy(feat_of[q][:], feat_f_of[q][:])
 
         def hidden(t):
             if not 0 <= t < NT:
                 return
             feat = feat_of[t // BLOCKS_IN_PIECE]
             tokens = slice((t % BLOCKS_IN_PIECE) * P, (t % BLOCKS_IN_PIECE + 1) * P)
-            u_ps = psum_u.tile([P, H], F32, name="u_ps")
+            u_of[t] = psum_u.tile([P, H], F32, name="u_ps")
             for cb in range(CB):
-                nc.tensor.matmul(u_ps[:], feat[:, cb, tokens], w0_sb[:, cb, :], start=(cb == 0), stop=False)
-            nc.tensor.matmul(u_ps[:], ones[:], b0_rows[:], start=False, stop=True)
-            stats = small.tile([P, 6], F32, name="stats")
-            nc.vector.bn_stats(stats[:], u_ps[:])
-            mean_var = small.tile([P, 2], F32, name="mean_var")
-            nc.vector.bn_aggr(mean_var[:], stats[:])
-            rstd = small.tile([P, 1], F32, name="rstd")
-            nc.scalar.activation(rstd[:], mean_var[:, 1:2], ACT.Abs_reciprocal_sqrt, bias=eps[:])
-            u_of[t], mean_var_of[t], rstd_of[t] = u_ps, mean_var, rstd
+                nc.tensor.matmul(u_of[t][:], feat[:, cb, tokens], w0_sb[:, cb, :], start=(cb == 0), stop=False)
+            nc.tensor.matmul(u_of[t][:], ones[:], b0_rows[:], start=False, stop=True)
+
+        def statistics(t):
+            if not 0 <= t < NT:
+                return
+            stats_of[t] = small.tile([P, 6], F32, name="stats")
+            nc.vector.bn_stats(stats_of[t][:], u_of[t][:])
+
+        def mean_and_variance(t):
+            if not 0 <= t < NT:
+                return
+            mean_var_of[t] = small.tile([P, 2], F32, name="mean_var")
+            nc.vector.bn_aggr(mean_var_of[t][:], stats_of[t][:])
+
+        def inverse_deviation(t):
+            if not 0 <= t < NT:
+                return
+            rstd_of[t] = small.tile([P, 1], F32, name="rstd")
+            nc.scalar.activation(rstd_of[t][:], mean_var_of[t][:, 1:2], ACT.Abs_reciprocal_sqrt, bias=eps[:])
 
         def offset(t):
             if not 0 <= t < NT:
                 return
-            minus = small.tile([P, 1], F32, name="minus")
-            nc.vector.tensor_scalar(minus[:], mean_var_of[t][:, 0:1], rstd_of[t][:], -1.0, ALU.mult, ALU.mult)
-            offset_of[t] = minus
+            offset_of[t] = small.tile([P, 1], F32, name="minus")
+            nc.vector.tensor_scalar(
+                offset_of[t][:], mean_var_of[t][:, 0:1], rstd_of[t][:], -1.0, ALU.mult, ALU.mult
+            )
 
         def normalise(t):
             if not 0 <= t < NT:
                 return
-            x_hat = work.tile([P, H], F32, name="x_hat")
-            nc.scalar.activation(x_hat[:], u_of[t][:], ACT.Identity, bias=offset_of[t][:], scale=rstd_of[t][:])
-            x_hat_of[t] = x_hat
+            x_hat_of[t] = work.tile([P, H], F32, name="x_hat")
+            nc.scalar.activation(
+                x_hat_of[t][:], u_of[t][:], ACT.Identity, bias=offset_of[t][:], scale=rstd_of[t][:]
+            )
+
+        def flip(t):
+            if not 0 <= t < NT:
+                return
+            flipped_of[t] = psum_t.tile([P, HB, P], F32, tag="flipped", name="flipped")
+            for hb in range(HB):
+                nc.tensor.transpose(flipped_of[t][:, hb, :], x_hat_of[t][:, hb * P : (hb + 1) * P], ident[:])
 
         def activate(t):
             if not 0 <= t < NT:
@@ -186,12 +206,9 @@ def tile_maplatentencoder_kernel(
             if t % BLOCKS_IN_CHUNK == 0:
                 m_of[ch] = work.tile([P, HB, CHUNK], BF16, name="m")
             tokens = slice((t % BLOCKS_IN_CHUNK) * P, (t % BLOCKS_IN_CHUNK + 1) * P)
-            flipped = psum_t.tile([P, HB, P], F32, tag="flipped", name="flipped")
-            for hb in range(HB):
-                nc.tensor.transpose(flipped[:, hb, :], x_hat_of[t][:, hb * P : (hb + 1) * P], ident[:])
             for hb in range(HB):
                 nc.scalar.activation(
-                    m_of[ch][:, hb, tokens], flipped[:, hb, :], ACT.Relu, bias=shift_col[hb], scale=gain_col[hb]
+                    m_of[ch][:, hb, tokens], flipped_of[t][:, hb, :], ACT.Relu, bias=shift_col[hb], scale=gain_col[hb]
                 )
 
         def project(j):
@@ -201,36 +218,45 @@ def tile_maplatentencoder_kernel(
             for n in range(part * PER_STEP, (part + 1) * PER_STEP):
                 db, hb = divmod(n, HB)
                 if hb == 0:
-                    o_of[db] = psum_o.tile([P, CHUNK], F32, name="o_ps")
+                    o_of[ch, db] = psum_o.tile([P, CHUNK], F32, name="o_ps")
                 nc.tensor.matmul(
-                    o_of[db][:],
+                    o_of[ch, db][:],
                     w1_sb[:, hb, db * P : (db + 1) * P],
                     m_of[ch][:, hb, :],
                     start=(hb == 0),
                     stop=(hb == HB - 1),
                 )
+
+        def store(j):
+            if not 0 <= j < NT:
+                return
+            ch, part = divmod(j, BLOCKS_IN_CHUNK)
+            for n in range(part * PER_STEP, (part + 1) * PER_STEP):
+                db, hb = divmod(n, HB)
                 if hb == HB - 1:
                     o_sb = work.tile([P, CHUNK], F32, name="o_sb")
                     if db == 0:
-                        nc.vector.tensor_scalar_add(o_sb[:], o_of[db][:], b1_col[db])
+                        nc.vector.tensor_scalar_add(o_sb[:], o_of[ch, db][:], b1_col[db])
                     else:
-                        nc.scalar.activation(o_sb[:], o_of[db][:], ACT.Identity, bias=b1_col[db])
+                        nc.scalar.activation(o_sb[:], o_of[ch, db][:], ACT.Identity, bias=b1_col[db])
                     nc.sync.dma_start(out[db * P : (db + 1) * P, ch * CHUNK : (ch + 1) * CHUNK], o_sb[:])
 
         def step(k):
-            normalise(k + AHEAD - 1)
-            hidden(k + AHEAD)
-            look_up(k + FEAT_AHEAD)
-            offset(k + AHEAD)
+            statistics(k + 3)
+            normalise(k + 2)
+            round_feat(k + 7)
+            mean_and_variance(k + 3)
+            inverse_deviation(k + 3)
+            flip(k)
+            look_up(k + 8)
+            store(k - 7)
+            add_positions(k + 9)
+            offset(k + 3)
+            project(k - 5)
+            hidden(k + 5)
             activate(k)
-            project(k - BEHIND)
 
-        add_positions(0)
-        add_positions(1)
-        for i in range(FEAT_AHEAD - AHEAD):
-            look_up(i)
-        for k in range(-AHEAD, 0):
-            step(k)
-        columns()
-        for k in range(0, NT + BEHIND):
+        for k in range(-9, NT + 7):
+            if k == 0:
+                columns()
             step(k)

@@ -17,7 +17,7 @@ NT = N // P
 PIECE = 256
 NQ = N // PIECE
 BLOCKS_IN_PIECE = PIECE // P
-CHUNK = 512
+CHUNK = 256
 BLOCKS_IN_CHUNK = CHUNK // P
 LN_EPS = 1e-5
 PER_STEP = CB * HB // BLOCKS_IN_CHUNK
@@ -235,28 +235,25 @@ def tile_maplatentencoder_kernel(
                 db, hb = divmod(n, HB)
                 if hb == HB - 1:
                     o_sb = work.tile([P, CHUNK], F32, name="o_sb")
-                    if db == 0:
-                        nc.vector.tensor_scalar_add(o_sb[:], o_of[ch, db][:], b1_col[db])
-                    else:
-                        nc.scalar.activation(o_sb[:], o_of[ch, db][:], ACT.Identity, bias=b1_col[db])
+                    nc.vector.tensor_scalar_add(o_sb[:], o_of[ch, db][:], b1_col[db])
                     nc.sync.dma_start(out[db * P : (db + 1) * P, ch * CHUNK : (ch + 1) * CHUNK], o_sb[:])
 
         def step(k):
-            statistics(k + 3)
+            flip(k)
+            project(k - 3)
             normalise(k + 2)
+            hidden(k + 5)
+            add_positions(k + 9)
+            statistics(k + 3)
             round_feat(k + 7)
             mean_and_variance(k + 3)
             inverse_deviation(k + 3)
-            flip(k)
+            store(k - 4)
             look_up(k + 8)
-            store(k - 7)
-            add_positions(k + 9)
             offset(k + 3)
-            project(k - 5)
-            hidden(k + 5)
             activate(k)
 
-        for k in range(-9, NT + 7):
+        for k in range(-9, NT + 4):
             if k == 0:
                 columns()
             step(k)

@@ -20,7 +20,8 @@ BLOCKS_IN_PIECE = PIECE // P
 CHUNK = 256
 BLOCKS_IN_CHUNK = CHUNK // P
 LN_EPS = 1e-5
-PER_STEP = CB * HB // BLOCKS_IN_CHUNK
+FIRST_ON_VECTOR = NT - 3
+assert BLOCKS_IN_CHUNK == CB
 
 FLOPS = 2 * N * C * H + 2 * N * H * C
 
@@ -37,6 +38,7 @@ def tile_maplatentencoder_kernel(
         held = ctx.enter_context(tc.tile_pool(name="held", bufs=1))
         loads = ctx.enter_context(tc.tile_pool(name="loads", bufs=NQ))
         work = ctx.enter_context(tc.tile_pool(name="work", bufs=4))
+        outs = ctx.enter_context(tc.tile_pool(name="outs", bufs=8))
         small = ctx.enter_context(tc.tile_pool(name="small", bufs=6))
         psum_u = ctx.enter_context(tc.psum_pool(name="psum_u", bufs=4))
         psum_t = ctx.enter_context(tc.psum_pool(name="psum_t", bufs=2))
@@ -177,7 +179,7 @@ def tile_maplatentencoder_kernel(
             nc.scalar.activation(rstd_of[t][:], mean_var_of[t][:, 1:2], ACT.Abs_reciprocal_sqrt, bias=eps[:])
 
         def offset(t):
-            if not 0 <= t < NT:
+            if not 0 <= t < FIRST_ON_VECTOR:
                 return
             offset_of[t] = small.tile([P, 1], F32, name="minus")
             nc.vector.tensor_scalar(
@@ -188,9 +190,14 @@ def tile_maplatentencoder_kernel(
             if not 0 <= t < NT:
                 return
             x_hat_of[t] = work.tile([P, H], F32, name="x_hat")
-            nc.scalar.activation(
-                x_hat_of[t][:], u_of[t][:], ACT.Identity, bias=offset_of[t][:], scale=rstd_of[t][:]
-            )
+            if t < FIRST_ON_VECTOR:
+                nc.scalar.activation(
+                    x_hat_of[t][:], u_of[t][:], ACT.Identity, bias=offset_of[t][:], scale=rstd_of[t][:]
+                )
+            else:
+                nc.vector.tensor_scalar(
+                    x_hat_of[t][:], u_of[t][:], mean_var_of[t][:, 0:1], rstd_of[t][:], ALU.subtract, ALU.mult
+                )
 
         def flip(t):
             if not 0 <= t < NT:
@@ -214,13 +221,12 @@ def tile_maplatentencoder_kernel(
         def project(j):
             if not 0 <= j < NT:
                 return
-            ch, part = divmod(j, BLOCKS_IN_CHUNK)
-            for n in range(part * PER_STEP, (part + 1) * PER_STEP):
-                db, hb = divmod(n, HB)
-                if hb == 0:
-                    o_of[ch, db] = psum_o.tile([P, CHUNK], F32, name="o_ps")
+            ch, db = divmod(j, BLOCKS_IN_CHUNK)
+            if db == 0:
+                o_of[ch] = psum_o.tile([P, CB, CHUNK], F32, name="o_ps")
+            for hb in range(HB):
                 nc.tensor.matmul(
-                    o_of[ch, db][:],
+                    o_of[ch][:, db, :],
                     w1_sb[:, hb, db * P : (db + 1) * P],
                     m_of[ch][:, hb, :],
                     start=(hb == 0),
@@ -230,30 +236,27 @@ def tile_maplatentencoder_kernel(
         def store(j):
             if not 0 <= j < NT:
                 return
-            ch, part = divmod(j, BLOCKS_IN_CHUNK)
-            for n in range(part * PER_STEP, (part + 1) * PER_STEP):
-                db, hb = divmod(n, HB)
-                if hb == HB - 1:
-                    o_sb = work.tile([P, CHUNK], F32, name="o_sb")
-                    nc.vector.tensor_scalar_add(o_sb[:], o_of[ch, db][:], b1_col[db])
-                    nc.sync.dma_start(out[db * P : (db + 1) * P, ch * CHUNK : (ch + 1) * CHUNK], o_sb[:])
+            ch, db = divmod(j, BLOCKS_IN_CHUNK)
+            o_sb = outs.tile([P, CHUNK], F32, name="o_sb")
+            nc.vector.tensor_scalar_add(o_sb[:], o_of[ch][:, db, :], b1_col[db])
+            nc.sync.dma_start(out[db * P : (db + 1) * P, ch * CHUNK : (ch + 1) * CHUNK], o_sb[:])
 
         def step(k):
             flip(k)
             project(k - 3)
             normalise(k + 2)
-            hidden(k + 5)
-            add_positions(k + 9)
+            round_feat(k + 8)
+            hidden(k + 6)
+            add_positions(k + 10)
             statistics(k + 3)
-            round_feat(k + 7)
             mean_and_variance(k + 3)
             inverse_deviation(k + 3)
             store(k - 4)
-            look_up(k + 8)
+            look_up(k + 9)
             offset(k + 3)
             activate(k)
 
-        for k in range(-9, NT + 4):
+        for k in range(-10, NT + 4):
             if k == 0:
                 columns()
             step(k)

@@ -44,33 +44,32 @@ def tile_maplatentencoder_kernel(
         psum_t = ctx.enter_context(tc.psum_pool(name="psum_t", bufs=2))
         psum_o = ctx.enter_context(tc.psum_pool(name="psum_o", bufs=2))
 
-        b0_as_rows = held.tile([P, P], F32, name="b0_as_rows")
-        nc.gpsimd.memset(b0_as_rows[:], 0.0)
         rows = held.tile([P, P], F32, name="rows")
         nc.gpsimd.memset(rows[:], 0.0)
         code_bf = [held.tile([P, S], BF16, name=f"code_bf{cb}") for cb in range(CB)]
-        nc.scalar.dma_start(code_bf[0][:], codebook[0:P, :])
-        nc.scalar.dma_start(b0_as_rows[0:HB, :], as_rows(b0))
-        w0_sb = held.tile([P, CB, H], BF16, name="w0_sb")
-        nc.scalar.dma_start(w0_sb[:], w0.rearrange("(cb p) h -> p cb h", p=P))
-
         map_view = map_pos.rearrange("(cb p) n -> p cb n", p=P)
         ego_view = ego_pos.rearrange("(cb p) n -> p cb n", p=P)
         map_sb, ego_sb = [], []
 
         def load_piece(q):
             tokens = slice(q * PIECE, (q + 1) * PIECE)
-            ego_t = loads.tile([P, CB, PIECE], F32, name="ego_t")
-            nc.sync.dma_start(ego_t[:], ego_view[:, :, tokens])
-            map_t = loads.tile([P, CB, PIECE], BF16, name="map_t")
-            nc.sync.dma_start(map_t[:], map_view[:, :, tokens])
-            map_sb.append(map_t)
-            ego_sb.append(ego_t)
+            nc.sync.dma_start(map_sb[q][:], map_view[:, :, tokens])
+            nc.sync.dma_start(ego_sb[q][:], ego_view[:, :, tokens])
 
-        nc.sync.dma_start(code_bf[1][:], codebook[P : 2 * P, :])
-        load_piece(0)
+        for q in range(NQ):
+            ego_sb.append(loads.tile([P, CB, PIECE], F32, name="ego_t"))
+            map_sb.append(loads.tile([P, CB, PIECE], BF16, name="map_t"))
+
+        b0_cols = held.tile([P, HB], F32, name="b0_cols")
+        nc.sync.dma_start(b0_cols[:], b0.rearrange("(b p) o -> p (b o)", p=P))
+        nc.sync.dma_start(code_bf[0][:], codebook[0:P, :])
+        nc.sync.dma_start(map_sb[0][:], map_view[:, :, 0:PIECE])
         offsets = held.tile([P, N // 16], U16, name="offsets")
         nc.sync.dma_start(offsets[:], offs)
+        nc.sync.dma_start(code_bf[1][:], codebook[P : 2 * P, :])
+        nc.sync.dma_start(ego_sb[0][:], ego_view[:, :, 0:PIECE])
+        w0_sb = held.tile([P, CB, H], BF16, name="w0_sb")
+        nc.sync.dma_start(w0_sb[:], w0.rearrange("(cb p) h -> p cb h", p=P))
         load_piece(1)
         load_piece(2)
         nc.sync.dma_start(rows[0:HB, :], as_rows(gain))
@@ -86,23 +85,24 @@ def tile_maplatentencoder_kernel(
         make_identity(nc, ident[:])
         ident_bf = held.tile([P, P], BF16, name="ident_bf")
         make_identity(nc, ident_bf[:])
-        ones = held.tile([P, P], BF16, name="ones")
-        nc.vector.memset(ones[:], 1.0)
         eps = held.tile([P, 1], F32, name="eps")
         nc.vector.memset(eps[:], LN_EPS)
+        first_rstd = held.tile([P, 1], F32, name="first_rstd")
+        nc.scalar.activation(first_rstd[:], eps[:], ACT.Abs_reciprocal_sqrt)
+        ones = held.tile([P, P], BF16, name="ones")
+        nc.vector.memset(ones[:], 1.0)
         b0_rows = held.tile([P, H], BF16, name="b0_rows")
         nc.vector.memset(b0_rows[:], 0.0)
 
         window = [held.tile([P, S], F32, name=f"window{cb}") for cb in range(CB)]
         nc.vector.tensor_copy(window[0][:], code_bf[0][:])
-        nc.scalar.copy(window[1][:], code_bf[1][:])
+        nc.scalar.copy(window[1][:, 0 : S // 2], code_bf[1][:, 0 : S // 2])
+        nc.vector.tensor_copy(window[1][:, S // 2 : S], code_bf[1][:, S // 2 : S])
 
-        b0_cols = psum_t.tile([P, P], F32, tag="flipped", name="b0_cols")
-        nc.tensor.transpose(b0_cols[:], b0_as_rows[:], ident[:])
         parts = held.tile([P, HB, 3], BF16, name="parts")
         rest = held.tile([P, HB], F32, name="rest")
-        nc.vector.tensor_copy(parts[:, :, 0], b0_cols[:, 0:HB])
-        nc.vector.tensor_tensor(rest[:], b0_cols[:, 0:HB], parts[:, :, 0], ALU.subtract)
+        nc.vector.tensor_copy(parts[:, :, 0], b0_cols[:])
+        nc.vector.tensor_tensor(rest[:], b0_cols[:], parts[:, :, 0], ALU.subtract)
         nc.vector.tensor_copy(parts[:, :, 1], rest[:])
         nc.vector.tensor_tensor(parts[:, :, 2], rest[:], parts[:, :, 1], ALU.subtract)
         b0_ps = psum_t.tile([P, H], F32, tag="flipped", name="b0_ps")
@@ -112,7 +112,7 @@ def tile_maplatentencoder_kernel(
             )
         nc.scalar.copy(b0_rows[0:3, :], b0_ps[0:3, :])
 
-        pos_of, feat_f_of, feat_of = {}, {}, {}
+        map_f_of, sum_of, feat_of = {}, {}, {}
         u_of, stats_of, mean_var_of, rstd_of, offset_of, x_hat_of, flipped_of, m_of, o_of = {}, {}, {}, {}, {}, {}, {}, {}, {}
         cols = held.tile([P, 2 * HB + CB], F32, name="cols")
         gain_col = [cols[:, hb : hb + 1] for hb in range(HB)]
@@ -124,31 +124,32 @@ def tile_maplatentencoder_kernel(
             nc.tensor.transpose(cols_ps[:], rows[:], ident[:])
             nc.vector.tensor_copy(cols[:], cols_ps[:, 0 : 2 * HB + CB])
 
-        def add_positions(i):
+        def cast_map(i):
             q, cb = divmod(i, CB)
             if not 0 <= q < NQ:
                 return
             if cb == 0:
-                pos_of[q] = work.tile([P, CB, PIECE], F32, name="pos")
-            nc.gpsimd.tensor_tensor(pos_of[q][:, cb, :], map_sb[q][:, cb, :], ego_sb[q][:, cb, :], ALU.add)
+                map_f_of[q] = loads.tile([P, CB, PIECE], F32, name="map_f")
+            nc.scalar.copy(map_f_of[q][:, cb, :], map_sb[q][:, cb, :])
 
         def look_up(i):
             q, cb = divmod(i, CB)
             if not 0 <= q < NQ:
                 return
             if cb == 0:
-                feat_f_of[q] = work.tile([P, CB, PIECE], F32, name="feat_f")
+                sum_of[q] = work.tile([P, CB, PIECE], F32, name="code_and_map")
             piece = offsets[:, q * (PIECE // 16) : (q + 1) * (PIECE // 16)]
             nc.vector.tensor_tensor(
-                feat_f_of[q][:, cb, :], window[cb][:].indirect(piece), pos_of[q][:, cb, :], ALU.add
+                sum_of[q][:, cb, :], window[cb][:].indirect(piece), map_f_of[q][:, cb, :], ALU.add
             )
 
-        def round_feat(i):
+        def add_ego(i):
             q, cb = divmod(i, CB)
-            if not 0 <= q < NQ or cb != CB - 1:
+            if not 0 <= q < NQ:
                 return
-            feat_of[q] = work.tile([P, CB, PIECE], BF16, name="feat")
-            nc.vector.tensor_copy(feat_of[q][:], feat_f_of[q][:])
+            if cb == 0:
+                feat_of[q] = work.tile([P, CB, PIECE], BF16, name="feat")
+            nc.gpsimd.tensor_tensor(feat_of[q][:, cb, :], sum_of[q][:, cb, :], ego_sb[q][:, cb, :], ALU.add)
 
         def hidden(t):
             if not 0 <= t < NT:
@@ -245,9 +246,9 @@ def tile_maplatentencoder_kernel(
             flip(k)
             project(k - 3)
             normalise(k + 2)
-            round_feat(k + 8)
+            add_ego(k + 8)
             hidden(k + 6)
-            add_positions(k + 10)
+            cast_map(k + 10)
             statistics(k + 3)
             mean_and_variance(k + 3)
             inverse_deviation(k + 3)

@@ -17,6 +17,7 @@ NT = N // P
 PIECE = 256
 NQ = N // PIECE
 BLOCKS_IN_PIECE = PIECE // P
+PIECES_IN_FLIGHT = 3
 CHUNK = 256
 BLOCKS_IN_CHUNK = CHUNK // P
 LN_EPS = 1e-5
@@ -37,6 +38,7 @@ def tile_maplatentencoder_kernel(
     with ExitStack() as ctx:
         held = ctx.enter_context(tc.tile_pool(name="held", bufs=1))
         loads = ctx.enter_context(tc.tile_pool(name="loads", bufs=NQ))
+        sums = ctx.enter_context(tc.tile_pool(name="sums", bufs=PIECES_IN_FLIGHT))
         work = ctx.enter_context(tc.tile_pool(name="work", bufs=4))
         outs = ctx.enter_context(tc.tile_pool(name="outs", bufs=8))
         small = ctx.enter_context(tc.tile_pool(name="small", bufs=6))
@@ -51,10 +53,11 @@ def tile_maplatentencoder_kernel(
         ego_view = ego_pos.rearrange("(cb p) n -> p cb n", p=P)
         map_sb, ego_sb = [], []
 
-        def load_piece(q):
-            tokens = slice(q * PIECE, (q + 1) * PIECE)
-            nc.sync.dma_start(map_sb[q][:], map_view[:, :, tokens])
-            nc.sync.dma_start(ego_sb[q][:], ego_view[:, :, tokens])
+        def load_map(q):
+            nc.sync.dma_start(map_sb[q][:], map_view[:, :, q * PIECE : (q + 1) * PIECE])
+
+        def load_ego(q):
+            nc.sync.dma_start(ego_sb[q][:], ego_view[:, :, q * PIECE : (q + 1) * PIECE])
 
         for q in range(NQ):
             ego_sb.append(loads.tile([P, CB, PIECE], F32, name="ego_t"))
@@ -63,23 +66,28 @@ def tile_maplatentencoder_kernel(
         b0_cols = held.tile([P, HB], F32, name="b0_cols")
         nc.sync.dma_start(b0_cols[:], b0.rearrange("(b p) o -> p (b o)", p=P))
         nc.sync.dma_start(code_bf[0][:], codebook[0:P, :])
-        nc.sync.dma_start(map_sb[0][:], map_view[:, :, 0:PIECE])
+        load_map(0)
         offsets = held.tile([P, N // 16], U16, name="offsets")
         nc.sync.dma_start(offsets[:], offs)
         nc.sync.dma_start(code_bf[1][:], codebook[P : 2 * P, :])
-        nc.sync.dma_start(ego_sb[0][:], ego_view[:, :, 0:PIECE])
+        load_ego(0)
         w0_sb = held.tile([P, CB, H], BF16, name="w0_sb")
         nc.sync.dma_start(w0_sb[:], w0.rearrange("(cb p) h -> p cb h", p=P))
-        load_piece(1)
-        load_piece(2)
+        load_map(1)
+        load_ego(1)
+        load_map(2)
+        load_map(3)
+        load_ego(2)
+        for q in range(4, NQ):
+            load_map(q)
         nc.sync.dma_start(rows[0:HB, :], as_rows(gain))
         nc.sync.dma_start(rows[HB : 2 * HB, :], as_rows(shift))
         nc.sync.dma_start(rows[2 * HB : 2 * HB + CB, :], as_rows(b1))
-        load_piece(3)
+        load_ego(3)
         w1_sb = held.tile([P, HB, C], BF16, name="w1_sb")
         nc.sync.dma_start(w1_sb[:], w1.rearrange("(hb p) d -> p hb d", p=P))
         for q in range(4, NQ):
-            load_piece(q)
+            load_ego(q)
 
         ident = held.tile([P, P], F32, name="ident")
         make_identity(nc, ident[:])
@@ -137,10 +145,13 @@ def tile_maplatentencoder_kernel(
             if not 0 <= q < NQ:
                 return
             if cb == 0:
-                sum_of[q] = work.tile([P, CB, PIECE], F32, name="code_and_map")
+                sum_of[q] = sums.tile([P, CB * PIECE + 2 * BLOCKS_IN_PIECE], F32, name="code_and_map")
             piece = offsets[:, q * (PIECE // 16) : (q + 1) * (PIECE // 16)]
             nc.vector.tensor_tensor(
-                sum_of[q][:, cb, :], window[cb][:].indirect(piece), map_f_of[q][:, cb, :], ALU.add
+                sum_of[q][:, cb * PIECE : (cb + 1) * PIECE],
+                window[cb][:].indirect(piece),
+                map_f_of[q][:, cb, :],
+                ALU.add,
             )
 
         def add_ego(i):
@@ -149,7 +160,8 @@ def tile_maplatentencoder_kernel(
                 return
             if cb == 0:
                 feat_of[q] = work.tile([P, CB, PIECE], BF16, name="feat")
-            nc.gpsimd.tensor_tensor(feat_of[q][:, cb, :], sum_of[q][:, cb, :], ego_sb[q][:, cb, :], ALU.add)
+            code_and_map = sum_of[q][:, cb * PIECE : (cb + 1) * PIECE]
+            nc.gpsimd.tensor_tensor(feat_of[q][:, cb, :], code_and_map, ego_sb[q][:, cb, :], ALU.add)
 
         def hidden(t):
             if not 0 <= t < NT:
@@ -170,8 +182,10 @@ def tile_maplatentencoder_kernel(
         def mean_and_variance(t):
             if not 0 <= t < NT:
                 return
-            mean_var_of[t] = small.tile([P, 2], F32, name="mean_var")
-            nc.vector.bn_aggr(mean_var_of[t][:], stats_of[t][:])
+            q, b = divmod(t, BLOCKS_IN_PIECE)
+            first = CB * PIECE + 2 * b
+            mean_var_of[t] = sum_of[q][:, first : first + 2]
+            nc.vector.bn_aggr(mean_var_of[t], stats_of[t][:])
 
         def inverse_deviation(t):
             if not 0 <= t < NT:

@@ -64,7 +64,7 @@ def tile_maplatentencoder_kernel(
             map_sb.append(loads.tile([P, CB, PIECE], BF16, name="map_t"))
 
         b0_cols = held.tile([P, HB], F32, name="b0_cols")
-        nc.sync.dma_start(b0_cols[:], b0.rearrange("(b p) o -> p (b o)", p=P))
+        nc.sync.dma_start(b0_cols[:], b0.rearrange("(p b) o -> p (b o)", b=HB))
         nc.sync.dma_start(code_bf[0][:], codebook[0:P, :])
         load_map(0)
         offsets = held.tile([P, N // 16], U16, name="offsets")
@@ -110,15 +110,17 @@ def tile_maplatentencoder_kernel(
         parts = held.tile([P, HB, 3], BF16, name="parts")
         rest = held.tile([P, HB], F32, name="rest")
         nc.vector.tensor_copy(parts[:, :, 0], b0_cols[:])
+        nc.vector.tensor_tensor(parts[:, :, 1], b0_cols[:], parts[:, :, 0], ALU.subtract)
         nc.vector.tensor_tensor(rest[:], b0_cols[:], parts[:, :, 0], ALU.subtract)
-        nc.vector.tensor_copy(parts[:, :, 1], rest[:])
         nc.vector.tensor_tensor(parts[:, :, 2], rest[:], parts[:, :, 1], ALU.subtract)
         b0_ps = psum_t.tile([P, H], F32, tag="flipped", name="b0_ps")
         for hb in range(HB):
             nc.tensor.matmul(
                 b0_ps[0:3, hb * P : (hb + 1) * P], parts[:, hb, :], ident_bf[:], start=True, stop=True
             )
-        nc.scalar.copy(b0_rows[0:3, :], b0_ps[0:3, :])
+        nc.scalar.copy(
+            b0_rows[0:3, :].rearrange("k (p b) -> k p b", b=HB), b0_ps[0:3, :].rearrange("k (b p) -> k p b", b=HB)
+        )
 
         map_f_of, sum_of, feat_of = {}, {}, {}
         u_of, stats_of, mean_var_of, rstd_of, offset_of, x_hat_of, flipped_of, m_of, o_of = {}, {}, {}, {}, {}, {}, {}, {}, {}

@@ -259,8 +259,8 @@ def tile_maplatentencoder_kernel(
             nc.sync.dma_start(out[db * P : (db + 1) * P, ch * CHUNK : (ch + 1) * CHUNK], o_sb[:])
 
         def step(k):
-            flip(k)
             project(k - 3)
+            flip(k)
             normalise(k + 2)
             add_ego(k + 8)
             hidden(k + 6)

from contextlib import ExitStack

import concourse.mybir as mybir
from concourse.masks import make_identity

BF16 = mybir.dt.bfloat16
F32 = mybir.dt.float32
U16 = mybir.dt.uint16
ALU = mybir.AluOpType
ACT = mybir.ActivationFunctionType

P = 128
C, S, N, H = 256, 1024, 2048, 512
CB = C // P
HB = H // P
NT = N // P
PIECE = 256
NQ = N // PIECE
BLOCKS_IN_PIECE = PIECE // P
PIECES_IN_FLIGHT = 3
CHUNK = 256
BLOCKS_IN_CHUNK = CHUNK // P
LN_EPS = 1e-5
FIRST_ON_VECTOR = NT - 3
assert BLOCKS_IN_CHUNK == CB

FLOPS = 2 * N * C * H + 2 * N * H * C


def as_rows(vector):
    return vector.rearrange("(b p) o -> b (p o)", p=P)


def tile_maplatentencoder_kernel(
    tc, codebook, map_pos, ego_pos, w0, b0, gain, shift, w1, b1, offs, out
):
    nc = tc.nc
    with ExitStack() as ctx:
        held = ctx.enter_context(tc.tile_pool(name="held", bufs=1))
        loads = ctx.enter_context(tc.tile_pool(name="loads", bufs=NQ))
        sums = ctx.enter_context(tc.tile_pool(name="sums", bufs=PIECES_IN_FLIGHT))
        work = ctx.enter_context(tc.tile_pool(name="work", bufs=4))
        outs = ctx.enter_context(tc.tile_pool(name="outs", bufs=8))
        small = ctx.enter_context(tc.tile_pool(name="small", bufs=6))
        psum_u = ctx.enter_context(tc.psum_pool(name="psum_u", bufs=4))
        psum_t = ctx.enter_context(tc.psum_pool(name="psum_t", bufs=2))
        psum_o = ctx.enter_context(tc.psum_pool(name="psum_o", bufs=2))

        rows = held.tile([P, P], F32, name="rows")
        nc.gpsimd.memset(rows[:], 0.0)
        code_bf = [held.tile([P, S], BF16, name=f"code_bf{cb}") for cb in range(CB)]
        map_view = map_pos.rearrange("(cb p) n -> p cb n", p=P)
        ego_view = ego_pos.rearrange("(cb p) n -> p cb n", p=P)
        map_sb, ego_sb = [], []

        def load_map(q):
            nc.sync.dma_start(map_sb[q][:], map_view[:, :, q * PIECE : (q + 1) * PIECE])

        def load_ego(q):
            nc.sync.dma_start(ego_sb[q][:], ego_view[:, :, q * PIECE : (q + 1) * PIECE])

        for q in range(NQ):
            ego_sb.append(loads.tile([P, CB, PIECE], F32, name="ego_t"))
            map_sb.append(loads.tile([P, CB, PIECE], BF16, name="map_t"))

        b0_cols = held.tile([P, HB], F32, name="b0_cols")
        nc.sync.dma_start(b0_cols[:], b0.rearrange("(p b) o -> p (b o)", b=HB))
        nc.sync.dma_start(code_bf[0][:], codebook[0:P, :])
        load_map(0)
        offsets = held.tile([P, N // 16], U16, name="offsets")
        nc.sync.dma_start(offsets[:], offs)
        nc.sync.dma_start(code_bf[1][:], codebook[P : 2 * P, :])
        load_ego(0)
        w0_sb = held.tile([P, CB, H], BF16, name="w0_sb")
        nc.sync.dma_start(w0_sb[:], w0.rearrange("(cb p) h -> p cb h", p=P))
        load_map(1)
        load_ego(1)
        load_map(2)
        load_map(3)
        load_ego(2)
        for q in range(4, NQ):
            load_map(q)
        nc.sync.dma_start(rows[0:HB, :], as_rows(gain))
        nc.sync.dma_start(rows[HB : 2 * HB, :], as_rows(shift))
        nc.sync.dma_start(rows[2 * HB : 2 * HB + CB, :], as_rows(b1))
        load_ego(3)
        w1_sb = held.tile([P, HB, C], BF16, name="w1_sb")
        nc.sync.dma_start(w1_sb[:], w1.rearrange("(hb p) d -> p hb d", p=P))
        for q in range(4, NQ):
            load_ego(q)

        ident = held.tile([P, P], F32, name="ident")
        make_identity(nc, ident[:])
        ident_bf = held.tile([P, P], BF16, name="ident_bf")
        make_identity(nc, ident_bf[:])
        eps = held.tile([P, 1], F32, name="eps")
        nc.vector.memset(eps[:], LN_EPS)
        first_rstd = held.tile([P, 1], F32, name="first_rstd")
        nc.scalar.activation(first_rstd[:], eps[:], ACT.Abs_reciprocal_sqrt)
        ones = held.tile([P, P], BF16, name="ones")
        nc.vector.memset(ones[:], 1.0)
        b0_rows = held.tile([P, H], BF16, name="b0_rows")
        nc.vector.memset(b0_rows[:], 0.0)

        window = [held.tile([P, S], F32, name=f"window{cb}") for cb in range(CB)]
        nc.vector.tensor_copy(window[0][:], code_bf[0][:])
        nc.scalar.copy(window[1][:, 0 : S // 2], code_bf[1][:, 0 : S // 2])
        nc.vector.tensor_copy(window[1][:, S // 2 : S], code_bf[1][:, S // 2 : S])

        parts = held.tile([P, HB, 3], BF16, name="parts")
        rest = held.tile([P, HB], F32, name="rest")
        nc.vector.tensor_copy(parts[:, :, 0], b0_cols[:])
        nc.vector.tensor_tensor(parts[:, :, 1], b0_cols[:], parts[:, :, 0], ALU.subtract)
        nc.vector.tensor_tensor(rest[:], b0_cols[:], parts[:, :, 0], ALU.subtract)
        nc.vector.tensor_tensor(parts[:, :, 2], rest[:], parts[:, :, 1], ALU.subtract)
        b0_ps = psum_t.tile([P, H], F32, tag="flipped", name="b0_ps")
        for hb in range(HB):
            nc.tensor.matmul(
                b0_ps[0:3, hb * P : (hb + 1) * P], parts[:, hb, :], ident_bf[:], start=True, stop=True
            )
        nc.scalar.copy(
            b0_rows[0:3, :].rearrange("k (p b) -> k p b", b=HB), b0_ps[0:3, :].rearrange("k (b p) -> k p b", b=HB)
        )

        map_f_of, sum_of, feat_of = {}, {}, {}
        u_of, stats_of, mean_var_of, rstd_of, offset_of, x_hat_of, flipped_of, m_of, o_of = {}, {}, {}, {}, {}, {}, {}, {}, {}
        cols = held.tile([P, 2 * HB + CB], F32, name="cols")
        gain_col = [cols[:, hb : hb + 1] for hb in range(HB)]
        shift_col = [cols[:, HB + hb : HB + hb + 1] for hb in range(HB)]
        b1_col = [cols[:, 2 * HB + db : 2 * HB + db + 1] for db in range(CB)]

        def columns():
            cols_ps = psum_t.tile([P, P], F32, tag="flipped", name="cols_ps")
            nc.tensor.transpose(cols_ps[:], rows[:], ident[:])
            nc.vector.tensor_copy(cols[:], cols_ps[:, 0 : 2 * HB + CB])

        def cast_map(i):
            q, cb = divmod(i, CB)
            if not 0 <= q < NQ:
                return
            if cb == 0:
                map_f_of[q] = loads.tile([P, CB, PIECE], F32, name="map_f")
            nc.scalar.copy(map_f_of[q][:, cb, :], map_sb[q][:, cb, :])

        def look_up(i):
            q, cb = divmod(i, CB)
            if not 0 <= q < NQ:
                return
            if cb == 0:
                sum_of[q] = sums.tile([P, CB * PIECE + 2 * BLOCKS_IN_PIECE], F32, name="code_and_map")
            piece = offsets[:, q * (PIECE // 16) : (q + 1) * (PIECE // 16)]
            nc.vector.tensor_tensor(
                sum_of[q][:, cb * PIECE : (cb + 1) * PIECE],
                window[cb][:].indirect(piece),
                map_f_of[q][:, cb, :],
                ALU.add,
            )

        def add_ego(i):
            q, cb = divmod(i, CB)
            if not 0 <= q < NQ:
                return
            if cb == 0:
                feat_of[q] = work.tile([P, CB, PIECE], BF16, name="feat")
            code_and_map = sum_of[q][:, cb * PIECE : (cb + 1) * PIECE]
            nc.gpsimd.tensor_tensor(feat_of[q][:, cb, :], code_and_map, ego_sb[q][:, cb, :], ALU.add)

        def hidden(t):
            if not 0 <= t < NT:
                return
            feat = feat_of[t // BLOCKS_IN_PIECE]
            tokens = slice((t % BLOCKS_IN_PIECE) * P, (t % BLOCKS_IN_PIECE + 1) * P)
            u_of[t] = psum_u.tile([P, H], F32, name="u_ps")
            for cb in range(CB):
                nc.tensor.matmul(u_of[t][:], feat[:, cb, tokens], w0_sb[:, cb, :], start=(cb == 0), stop=False)
            nc.tensor.matmul(u_of[t][:], ones[:], b0_rows[:], start=False, stop=True)

        def statistics(t):
            if not 0 <= t < NT:
                return
            stats_of[t] = small.tile([P, 6], F32, name="stats")
            nc.vector.bn_stats(stats_of[t][:], u_of[t][:])

        def mean_and_variance(t):
            if not 0 <= t < NT:
                return
            q, b = divmod(t, BLOCKS_IN_PIECE)
            first = CB * PIECE + 2 * b
            mean_var_of[t] = sum_of[q][:, first : first + 2]
            nc.vector.bn_aggr(mean_var_of[t], stats_of[t][:])

        def inverse_deviation(t):
            if not 0 <= t < NT:
                return
            rstd_of[t] = small.tile([P, 1], F32, name="rstd")
            nc.scalar.activation(rstd_of[t][:], mean_var_of[t][:, 1:2], ACT.Abs_reciprocal_sqrt, bias=eps[:])

        def offset(t):
            if not 0 <= t < FIRST_ON_VECTOR:
                return
            offset_of[t] = small.tile([P, 1], F32, name="minus")
            nc.vector.tensor_scalar(
                offset_of[t][:], mean_var_of[t][:, 0:1], rstd_of[t][:], -1.0, ALU.mult, ALU.mult
            )

        def normalise(t):
            if not 0 <= t < NT:
                return
            x_hat_of[t] = work.tile([P, H], F32, name="x_hat")
            if t < FIRST_ON_VECTOR:
                nc.scalar.activation(
                    x_hat_of[t][:], u_of[t][:], ACT.Identity, bias=offset_of[t][:], scale=rstd_of[t][:]
                )
            else:
                nc.vector.tensor_scalar(
                    x_hat_of[t][:], u_of[t][:], mean_var_of[t][:, 0:1], rstd_of[t][:], ALU.subtract, ALU.mult
                )

        def flip(t):
            if not 0 <= t < NT:
                return
            flipped_of[t] = psum_t.tile([P, HB, P], F32, tag="flipped", name="flipped")
            for hb in range(HB):
                nc.tensor.transpose(flipped_of[t][:, hb, :], x_hat_of[t][:, hb * P : (hb + 1) * P], ident[:])

        def activate(t):
            if not 0 <= t < NT:
                return
            ch = t // BLOCKS_IN_CHUNK
            if t % BLOCKS_IN_CHUNK == 0:
                m_of[ch] = work.tile([P, HB, CHUNK], BF16, name="m")
            tokens = slice((t % BLOCKS_IN_CHUNK) * P, (t % BLOCKS_IN_CHUNK + 1) * P)
            for hb in range(HB):
                nc.scalar.activation(
                    m_of[ch][:, hb, tokens], flipped_of[t][:, hb, :], ACT.Relu, bias=shift_col[hb], scale=gain_col[hb]
                )

        def project(j):
            if not 0 <= j < NT:
                return
            ch, db = divmod(j, BLOCKS_IN_CHUNK)
            if db == 0:
                o_of[ch] = psum_o.tile([P, CB, CHUNK], F32, name="o_ps")
            for hb in range(HB):
                nc.tensor.matmul(
                    o_of[ch][:, db, :],
                    w1_sb[:, hb, db * P : (db + 1) * P],
                    m_of[ch][:, hb, :],
                    start=(hb == 0),
                    stop=(hb == HB - 1),
                )

        def store(j):
            if not 0 <= j < NT:
                return
            ch, db = divmod(j, BLOCKS_IN_CHUNK)
            o_sb = outs.tile([P, CHUNK], F32, name="o_sb")
            nc.vector.tensor_scalar_add(o_sb[:], o_of[ch][:, db, :], b1_col[db])
            nc.sync.dma_start(out[db * P : (db + 1) * P, ch * CHUNK : (ch + 1) * CHUNK], o_sb[:])

        def step(k):
            project(k - 3)
            flip(k)
            normalise(k + 2)
            add_ego(k + 8)
            hidden(k + 6)
            cast_map(k + 10)
            statistics(k + 3)
            mean_and_variance(k + 3)
            inverse_deviation(k + 3)
            store(k - 4)
            look_up(k + 9)
            offset(k + 3)
            activate(k)

        for k in range(-10, NT + 4):
            if k == 0:
                columns()
            step(k)
